import numpy as np
import ml_dtypes


def mxq(x, axis, fmt="e4m3"):
    dtype, down = {"e4m3": (ml_dtypes.float8_e4m3fn, 7), "e5m2": (ml_dtypes.float8_e5m2, 14)}[fmt]
    v = np.moveaxis(np.asarray(x, np.float32).astype(ml_dtypes.bfloat16).astype(np.float64), axis, -1)
    blocks = v.reshape(v.shape[:-1] + (-1, 32))
    amax = np.abs(blocks).max(-1, keepdims=True)
    byte = np.maximum(np.where(amax > 0, np.frexp(amax)[1] - 1 + 127, 0) - down, 1)
    scale = np.exp2(byte - 127.0)
    codes = (blocks / scale).astype(np.float32).astype(dtype).astype(np.float64)
    return np.moveaxis((codes * scale).reshape(v.shape), -1, axis)


WIDE = False


def mx_kscale(k):
    if not WIDE:
        return np.ones(k)
    levels = np.array([10, -10, 5, -5, 0])
    a = np.random.permutation(np.resize(levels, k // 512 * 4)).reshape(k // 512, 4)
    idx = np.arange(k)
    return np.exp2(a[idx // 512, idx % 128 // 32])


BF16 = ml_dtypes.bfloat16


def bf(x):
    return np.asarray(x, np.float32).astype(BF16)


def f64(x):
    return np.asarray(x).astype(np.float64)


B, L, D, O = 2, 256, 512, 16


def setup_inputs():
    s, t = mx_kscale(D), mx_kscale(D)
    return {"input1": bf(np.random.standard_normal((B, L, D)) * s),
            "input2": bf(np.random.standard_normal((B, L, D)) / t),
            "w1": bf(np.random.standard_normal((D, O, D)) * (4.0 / D) / s[:, None, None] * t),
            "aff1": bf(np.random.standard_normal((B, L, O))),
            "aff2": bf(np.random.standard_normal((B, L, O))),
            "bias": bf(1.0 + 0.25 * np.random.standard_normal(O))}


def reference(input1, input2, w1, aff1, aff2, bias):
    u = mxq(f64(input1), 2, "e4m3").reshape(B * L, D) @ mxq(f64(w1), 0, "e4m3").reshape(D, O * D)
    u = u.reshape(B, L * O, D)
    p = mxq(u, 2, "e4m3") @ mxq(f64(input2), 2, "e4m3").transpose(0, 2, 1)
    logits_1 = p.reshape(B, L, O, L).transpose(0, 1, 3, 2)
    logits_2 = f64(aff1)[:, :, None, :] + f64(aff2)[:, None, :, :] + f64(bias)
    return logits_1 + logits_2

@@ -1,0 +1,239 @@
+from contextlib import ExitStack
+
+import concourse.mybir as mybir
+from concourse.masks import make_identity
+
+F32 = mybir.dt.float32
+BF16 = mybir.dt.bfloat16
+U32 = mybir.dt.uint32
+U8 = mybir.dt.uint8
+I32 = mybir.dt.int32
+FP8X4 = mybir.dt.float8_e4m3fn_x4
+ADD = mybir.AluOpType.add
+
+B, L, D, O = 2, 256, 512, 16
+P = 128
+PACK = 4
+NCH = (B * L) // P
+FLOPS = 2 * (B * L) * D * (O * D) + 2 * B * (L * O) * D * L
+
+MANUAL = True
+W_BUFS = 6
+REGROUP_AHEAD = 3
+QUANT_AHEAD = 2
+
+
+def tile_biaffine_2_pa_kernel(tc, input1, input2, w1, aff1, aff2, bias, out):
+    nc = tc.nc
+    with ExitStack() as ctx:
+        const = ctx.enter_context(tc.tile_pool(name="const", bufs=1))
+        wraw_pool = ctx.enter_context(tc.tile_pool(name="wraw", bufs=W_BUFS))
+        wg_pool = ctx.enter_context(tc.tile_pool(name="wg", bufs=3))
+        wq_pool = ctx.enter_context(tc.tile_pool(name="wq", bufs=4))
+        ug_pool = ctx.enter_context(tc.tile_pool(name="ug", bufs=3))
+        psum = ctx.enter_context(tc.psum_pool(name="psum", bufs=6))
+        psum_c = ctx.enter_context(tc.psum_pool(name="psumc", bufs=2))
+        if MANUAL:
+            ctx.enter_context(tc.manual_schedule())
+
+        ident = const.tile([P, P], BF16)
+        a1pad = const.tile([P, NCH, P], BF16)
+        bias_bc = const.tile([P, O], BF16)
+        sel = const.tile([P, O], BF16)
+        rmat = const.tile([P, L * O], BF16)
+        lmat = const.tile([P, NCH, P], BF16)
+        x1_raw = const.tile([P, NCH, D], BF16)
+        x2_raw = const.tile([P, NCH, D], BF16)
+        x1_g = const.tile([P, NCH * P, PACK], BF16, align_bytes=64)
+        x2_g = const.tile([P, NCH * P, PACK], BF16, align_bytes=64)
+        x1_c = const.tile([P, NCH * P], U32, align_bytes=64)
+        x1_s = const.tile([P, NCH * P], U8, align_bytes=64)
+        x2_c = const.tile([P, NCH * P], U32, align_bytes=64)
+        x2_s = const.tile([P, NCH * P], U8, align_bytes=64)
+        u_c = const.tile([P, O, NCH * P], U32, align_bytes=64)
+        u_s = const.tile([P, O, NCH * P], U8, align_bytes=64)
+        osb = [const.tile([P, L * O], F32, name="osb%d" % c) for c in range(NCH)]
+
+        w_view = w1.rearrange("(t p) o j -> p t o j", p=P)
+        w_raw = {}
+        w_g = {}
+        w_q = {}
+        u_g = {}
+
+        def load_w(o):
+            wr = wraw_pool.tile([P, PACK, D], BF16, name="wr", tag="wr")
+            nc.sync.dma_start(out=wr[:], in_=w_view[:, :, o, :])
+            w_raw[o] = wr
+
+        def regroup_w(o):
+            wg = wg_pool.tile([P, D, PACK], BF16, name="wg", tag="wg", align_bytes=64)
+            nc.vector.tensor_copy(
+                out=wg[:].rearrange("p (c i) t -> p c t i", i=4),
+                in_=w_raw[o][:].rearrange("p t (c i) -> p c t i", i=4),
+            )
+            w_g[o] = wg
+
+        def quant_w(o):
+            wc = wq_pool.tile([P, D], U32, name="wc", tag="wc", align_bytes=64)
+            ws = wq_pool.tile([P, D], U8, name="ws", tag="ws", align_bytes=64)
+            nc.vector.quantize_mx(
+                out=wc[:].bitcast(FP8X4),
+                scales=ws[:],
+                in_=w_g[o][:].rearrange("p c t -> p (c t)"),
+            )
+            w_q[o] = (wc, ws)
+
+        def transpose_tokens(raw, grouped, c):
+            xt = psum.tile([P, PACK, P], BF16, name="xt", tag="acc")
+            for t in range(PACK):
+                nc.tensor.transpose(xt[:, t, :], raw[:, c, t * P:(t + 1) * P], ident[:])
+            nc.scalar.copy(
+                out=grouped[:, c * P:(c + 1) * P, :],
+                in_=xt[:].rearrange("p t r -> p r t"),
+            )
+
+        def quant_tokens(grouped, codes, scales, c0, c1):
+            nc.vector.quantize_mx(
+                out=codes[:, c0 * P:c1 * P].bitcast(FP8X4),
+                scales=scales[:, c0 * P:c1 * P],
+                in_=grouped[:, c0 * P:c1 * P, :].rearrange("p r t -> p (r t)"),
+            )
+
+        def stage1(o):
+            wc, ws = w_q[o]
+            ug = ug_pool.tile([P, NCH * P, PACK], BF16, name="ug", tag="ug", align_bytes=64)
+            for c in range(NCH):
+                ub = psum.tile([P, PACK, P], F32, name="ub", tag="acc")
+                for t in range(PACK):
+                    nc.tensor.matmul_mx(
+                        out=ub[:, t, :],
+                        lhsT=wc[:, t * P:(t + 1) * P].bitcast(FP8X4),
+                        lhsT_scale=ws[:, t * P:(t + 1) * P],
+                        rhs=x1_c[:, c * P:(c + 1) * P].bitcast(FP8X4),
+                        rhs_scale=x1_s[:, c * P:(c + 1) * P],
+                        start=True,
+                        stop=True,
+                    )
+                nc.scalar.copy(
+                    out=ug[:, c * P:(c + 1) * P, :],
+                    in_=ub[:].rearrange("p t r -> p r t"),
+                )
+            u_g[o] = ug
+
+        def quant_u(o):
+            nc.vector.quantize_mx(
+                out=u_c[:, o, :].bitcast(FP8X4),
+                scales=u_s[:, o, :],
+                in_=u_g[o][:].rearrange("p r t -> p (r t)"),
+            )
+
+        def affine_quarter(m, q):
+            c, yh = divmod(m, 2)
+            s = yh * 4 + q
+            cb = psum_c.tile([P, 512], F32, name="cb", tag="cb")
+            nc.tensor.matmul(
+                out=cb[:],
+                lhsT=lmat[:, c, :],
+                rhs=rmat[:, s * 512:(s + 1) * 512],
+                start=True,
+                stop=True,
+            )
+            nc.scalar.copy(out=osb[c][:, s * 512:(s + 1) * 512], in_=cb[:])
+
+        def stage2(m):
+            c, yh = divmod(m, 2)
+            b, h = divmod(c, 2)
+            c2 = 2 * b + yh
+            half = L * O // 2
+            ov = osb[c][:, yh * half:(yh + 1) * half].rearrange("p (y o) -> p y o", o=O)
+            for g in range(4):
+                if m + 1 < 2 * NCH:
+                    affine_quarter(m + 1, g)
+                pb = psum.tile([P, 4, P], F32, name="pb", tag="acc")
+                for oo in range(4):
+                    o = 4 * g + oo
+                    nc.tensor.matmul_mx(
+                        out=pb[:, oo, :],
+                        lhsT=u_c[:, o, c * P:(c + 1) * P].bitcast(FP8X4),
+                        lhsT_scale=u_s[:, o, c * P:(c + 1) * P],
+                        rhs=x2_c[:, c2 * P:(c2 + 1) * P].bitcast(FP8X4),
+                        rhs_scale=x2_s[:, c2 * P:(c2 + 1) * P],
+                        start=True,
+                        stop=True,
+                    )
+                nc.vector.tensor_tensor(
+                    out=ov[:, :, 4 * g:4 * g + 4],
+                    in0=pb[:].rearrange("p o y -> p y o"),
+                    in1=ov[:, :, 4 * g:4 * g + 4],
+                    op=ADD,
+                )
+            nc.sync.dma_start(
+                out=out[b, h * P:(h + 1) * P, yh * P:(yh + 1) * P, :],
+                in_=ov,
+            )
+
+        make_identity(nc, ident[:])
+        nc.vector.memset(a1pad[:].bitcast(I32), 0)
+        load_w(0)
+        nc.sync.dma_start(out=x1_raw[:], in_=input1.rearrange("b (h p) i -> p (b h) i", p=P))
+        for o in range(1, W_BUFS):
+            load_w(o)
+        nc.scalar.dma_start(out=a1pad[:, :, 0:O], in_=aff1.rearrange("b (h p) o -> p (b h) o", p=P))
+        nc.scalar.dma_start(out=bias_bc[:], in_=bias.partition_broadcast(P))
+        nc.scalar.dma_start(out=x2_raw[:], in_=input2.rearrange("b (h p) i -> p (b h) i", p=P))
+
+        nc.vector.tensor_tensor(out=sel[:], in0=ident[:, 0:O], in1=ident[:, O:2 * O], op=ADD)
+        rview = rmat[:].rearrange("p (y o) -> p y o", o=O)
+        nc.vector.tensor_copy(
+            out=rview[:, 0:L // 2, :],
+            in_=sel[:].unsqueeze(1).to_broadcast([P, L // 2, O]),
+        )
+        nc.scalar.copy(
+            out=rview[:, L // 2:L, :],
+            in_=sel[:].unsqueeze(1).to_broadcast([P, L // 2, O]),
+        )
+        nc.gpsimd.dma_start(out=rmat[2 * O:2 * O + B, :], in_=aff2.rearrange("b y o -> b (y o)"))
+        nc.vector.tensor_copy(
+            out=a1pad[:, :, O:2 * O],
+            in_=bias_bc[:].unsqueeze(1).to_broadcast([P, NCH, O]),
+        )
+        for b in range(B):
+            nc.vector.memset(a1pad[:, 2 * b:2 * b + 2, 2 * O + b:2 * O + b + 1], 1.0)
+
+        for c in range(NCH):
+            transpose_tokens(x1_raw, x1_g, c)
+        regroup_w(0)
+        quant_w(0)
+        quant_tokens(x1_g, x1_c, x1_s, 0, 1)
+        quant_tokens(x1_g, x1_c, x1_s, 1, 2)
+        regroup_w(1)
+        quant_tokens(x1_g, x1_c, x1_s, 2, 3)
+        quant_tokens(x1_g, x1_c, x1_s, 3, 4)
+        quant_w(1)
+        regroup_w(2)
+
+        for s in range(O):
+            stage1(s)
+            if s < NCH:
+                transpose_tokens(x2_raw, x2_g, s)
+            if s == NCH:
+                lt = psum.tile([P, NCH, P], BF16, name="lt", tag="acc")
+                for c in range(NCH):
+                    nc.tensor.transpose(lt[:, c, :], a1pad[:, c, :], ident[:])
+                nc.scalar.copy(out=lmat[:], in_=lt[:])
+            if s + REGROUP_AHEAD < O:
+                regroup_w(s + REGROUP_AHEAD)
+            if s >= 1:
+                quant_u(s - 1)
+            if s + QUANT_AHEAD < O:
+                quant_w(s + QUANT_AHEAD)
+            if s + W_BUFS < O:
+                load_w(s + W_BUFS)
+            if s == NCH:
+                quant_tokens(x2_g, x2_c, x2_s, 0, NCH)
+            if s >= O - 4:
+                affine_quarter(0, s - (O - 4))
+        quant_u(O - 1)
+
+        for m in range(2 * NCH):
+            stage2(m)

@@ -19,8 +19,10 @@ FLOPS = 2 * (B * L) * D * (O * D) + 2 * B * (L * O) * D * L
 
 MANUAL = True
 W_BUFS = 6
+W_PREFETCH = 4
 REGROUP_AHEAD = 3
 QUANT_AHEAD = 2
+V_EVAC_FROM = 13
 
 
 def tile_biaffine_2_pa_kernel(tc, input1, input2, w1, aff1, aff2, bias, out):
@@ -114,10 +116,16 @@ def tile_biaffine_2_pa_kernel(tc, input1, input2, w1, aff1, aff2, bias, out):
                         start=True,
                         stop=True,
                     )
-                nc.scalar.copy(
-                    out=ug[:, c * P:(c + 1) * P, :],
-                    in_=ub[:].rearrange("p t r -> p r t"),
-                )
+                if o >= V_EVAC_FROM and c >= 2:
+                    nc.vector.tensor_copy(
+                        out=ug[:, c * P:(c + 1) * P, :],
+                        in_=ub[:].rearrange("p t r -> p r t"),
+                    )
+                else:
+                    nc.scalar.copy(
+                        out=ug[:, c * P:(c + 1) * P, :],
+                        in_=ub[:].rearrange("p t r -> p r t"),
+                    )
             u_g[o] = ug
 
         def quant_u(o):
@@ -140,46 +148,50 @@ def tile_biaffine_2_pa_kernel(tc, input1, input2, w1, aff1, aff2, bias, out):
             )
             nc.scalar.copy(out=osb[c][:, s * 512:(s + 1) * 512], in_=cb[:])
 
-        def stage2(m):
+        def out_view(m):
+            c, yh = divmod(m, 2)
+            half = L * O // 2
+            return osb[c][:, yh * half:(yh + 1) * half].rearrange("p (y o) -> p y o", o=O)
+
+        def stage2_group(m, g):
+            c, yh = divmod(m, 2)
+            c2 = 2 * (c // 2) + yh
+            ov = out_view(m)
+            pb = psum.tile([P, 4, P], F32, name="pb", tag="acc")
+            for oo in range(4):
+                o = 4 * g + oo
+                nc.tensor.matmul_mx(
+                    out=pb[:, oo, :],
+                    lhsT=u_c[:, o, c * P:(c + 1) * P].bitcast(FP8X4),
+                    lhsT_scale=u_s[:, o, c * P:(c + 1) * P],
+                    rhs=x2_c[:, c2 * P:(c2 + 1) * P].bitcast(FP8X4),
+                    rhs_scale=x2_s[:, c2 * P:(c2 + 1) * P],
+                    start=True,
+                    stop=True,
+                )
+            nc.vector.tensor_tensor(
+                out=ov[:, :, 4 * g:4 * g + 4],
+                in0=pb[:].rearrange("p o y -> p y o"),
+                in1=ov[:, :, 4 * g:4 * g + 4],
+                op=ADD,
+            )
+
+        def store(m):
             c, yh = divmod(m, 2)
             b, h = divmod(c, 2)
-            c2 = 2 * b + yh
-            half = L * O // 2
-            ov = osb[c][:, yh * half:(yh + 1) * half].rearrange("p (y o) -> p y o", o=O)
-            for g in range(4):
-                if m + 1 < 2 * NCH:
-                    affine_quarter(m + 1, g)
-                pb = psum.tile([P, 4, P], F32, name="pb", tag="acc")
-                for oo in range(4):
-                    o = 4 * g + oo
-                    nc.tensor.matmul_mx(
-                        out=pb[:, oo, :],
-                        lhsT=u_c[:, o, c * P:(c + 1) * P].bitcast(FP8X4),
-                        lhsT_scale=u_s[:, o, c * P:(c + 1) * P],
-                        rhs=x2_c[:, c2 * P:(c2 + 1) * P].bitcast(FP8X4),
-                        rhs_scale=x2_s[:, c2 * P:(c2 + 1) * P],
-                        start=True,
-                        stop=True,
-                    )
-                nc.vector.tensor_tensor(
-                    out=ov[:, :, 4 * g:4 * g + 4],
-                    in0=pb[:].rearrange("p o y -> p y o"),
-                    in1=ov[:, :, 4 * g:4 * g + 4],
-                    op=ADD,
-                )
             nc.sync.dma_start(
                 out=out[b, h * P:(h + 1) * P, yh * P:(yh + 1) * P, :],
-                in_=ov,
+                in_=out_view(m),
             )
 
         make_identity(nc, ident[:])
         nc.vector.memset(a1pad[:].bitcast(I32), 0)
-        load_w(0)
-        nc.sync.dma_start(out=x1_raw[:], in_=input1.rearrange("b (h p) i -> p (b h) i", p=P))
-        for o in range(1, W_BUFS):
-            load_w(o)
         nc.scalar.dma_start(out=a1pad[:, :, 0:O], in_=aff1.rearrange("b (h p) o -> p (b h) o", p=P))
         nc.scalar.dma_start(out=bias_bc[:], in_=bias.partition_broadcast(P))
+        load_w(0)
+        nc.sync.dma_start(out=x1_raw[:], in_=input1.rearrange("b (h p) i -> p (b h) i", p=P))
+        for o in range(1, W_PREFETCH):
+            load_w(o)
         nc.scalar.dma_start(out=x2_raw[:], in_=input2.rearrange("b (h p) i -> p (b h) i", p=P))
 
         nc.vector.tensor_tensor(out=sel[:], in0=ident[:, 0:O], in1=ident[:, O:2 * O], op=ADD)
@@ -193,47 +205,66 @@ def tile_biaffine_2_pa_kernel(tc, input1, input2, w1, aff1, aff2, bias, out):
             in_=sel[:].unsqueeze(1).to_broadcast([P, L // 2, O]),
         )
         nc.gpsimd.dma_start(out=rmat[2 * O:2 * O + B, :], in_=aff2.rearrange("b y o -> b (y o)"))
-        nc.vector.tensor_copy(
-            out=a1pad[:, :, O:2 * O],
-            in_=bias_bc[:].unsqueeze(1).to_broadcast([P, NCH, O]),
-        )
-        for b in range(B):
-            nc.vector.memset(a1pad[:, 2 * b:2 * b + 2, 2 * O + b:2 * O + b + 1], 1.0)
+
+        def regroup_and_prefetch(o):
+            regroup_w(o)
+            if o + W_PREFETCH < O:
+                load_w(o + W_PREFETCH)
 
         for c in range(NCH):
             transpose_tokens(x1_raw, x1_g, c)
-        regroup_w(0)
+        regroup_and_prefetch(0)
         quant_w(0)
         quant_tokens(x1_g, x1_c, x1_s, 0, 1)
         quant_tokens(x1_g, x1_c, x1_s, 1, 2)
-        regroup_w(1)
+        regroup_and_prefetch(1)
         quant_tokens(x1_g, x1_c, x1_s, 2, 3)
         quant_tokens(x1_g, x1_c, x1_s, 3, 4)
         quant_w(1)
-        regroup_w(2)
+        regroup_and_prefetch(2)
 
         for s in range(O):
-            stage1(s)
-            if s < NCH:
-                transpose_tokens(x2_raw, x2_g, s)
-            if s == NCH:
-                lt = psum.tile([P, NCH, P], BF16, name="lt", tag="acc")
-                for c in range(NCH):
-                    nc.tensor.transpose(lt[:, c, :], a1pad[:, c, :], ident[:])
-                nc.scalar.copy(out=lmat[:], in_=lt[:])
             if s + REGROUP_AHEAD < O:
-                regroup_w(s + REGROUP_AHEAD)
+                regroup_and_prefetch(s + REGROUP_AHEAD)
             if s >= 1:
                 quant_u(s - 1)
             if s + QUANT_AHEAD < O:
                 quant_w(s + QUANT_AHEAD)
-            if s + W_BUFS < O:
-                load_w(s + W_BUFS)
-            if s == NCH:
+            if s == 2:
+                nc.vector.tensor_copy(
+                    out=a1pad[:, :, O:2 * O],
+                    in_=bias_bc[:].unsqueeze(1).to_broadcast([P, NCH, O]),
+                )
+                for b in range(B):
+                    nc.vector.memset(a1pad[:, 2 * b:2 * b + 2, 2 * O + b:2 * O + b + 1], 1.0)
+            if 3 <= s < 3 + NCH:
+                transpose_tokens(x2_raw, x2_g, s - 3)
+            if s == 7:
                 quant_tokens(x2_g, x2_c, x2_s, 0, NCH)
-            if s >= O - 4:
-                affine_quarter(0, s - (O - 4))
+                lt = psum.tile([P, NCH, P], BF16, name="lt", tag="acc")
+                for c in range(NCH):
+                    nc.tensor.transpose(lt[:, c, :], a1pad[:, c, :], ident[:])
+                nc.scalar.copy(out=lmat[:], in_=lt[:])
+            if 9 <= s < 13:
+                affine_quarter(0, s - 9)
+            if s == 13:
+                affine_quarter(1, 0)
+                affine_quarter(1, 1)
+            if s == 14:
+                affine_quarter(1, 2)
+                stage2_group(0, 0)
+                stage2_group(0, 1)
+            if s == 15:
+                affine_quarter(1, 3)
+                stage2_group(0, 2)
+            stage1(s)
         quant_u(O - 1)
+        stage2_group(0, 3)
+        store(0)
 
-        for m in range(2 * NCH):
-            stage2(m)
+        for m in range(1, 2 * NCH):
+            for g in range(4):
+                if m + 1 < 2 * NCH:
+                    affine_quarter(m + 1, g)
+                stage2_group(m, g)
+            store(m)

@@ -15,23 +15,27 @@ B, L, D, O = 2, 256, 512, 16
 P = 128
 PACK = 4
 NCH = (B * L) // P
+NTOK = B * L
+UNITS = 2 * NCH
 FLOPS = 2 * (B * L) * D * (O * D) + 2 * B * (L * O) * D * L
 
 MANUAL = True
-W_BUFS = 6
-W_PREFETCH = 4
-REGROUP_AHEAD = 3
-QUANT_AHEAD = 2
+W_GROUPS = [[0], [1]] + [[o, o + 1] for o in range(2, O, 2)]
+U_GROUPS = [[o, o + 1] for o in range(0, O - 2, 2)] + [[O - 2], [O - 1]]
+W_PREFETCH = 3
 V_EVAC_FROM = 13
+AFFINE_EARLY = 2
+AFFINE_AHEAD = 3
+LAST_SPLIT = 2
 
 
 def tile_biaffine_2_pa_kernel(tc, input1, input2, w1, aff1, aff2, bias, out):
     nc = tc.nc
     with ExitStack() as ctx:
         const = ctx.enter_context(tc.tile_pool(name="const", bufs=1))
-        wraw_pool = ctx.enter_context(tc.tile_pool(name="wraw", bufs=W_BUFS))
-        wg_pool = ctx.enter_context(tc.tile_pool(name="wg", bufs=3))
-        wq_pool = ctx.enter_context(tc.tile_pool(name="wq", bufs=4))
+        wraw_pool = ctx.enter_context(tc.tile_pool(name="wraw", bufs=W_PREFETCH))
+        wg_pool = ctx.enter_context(tc.tile_pool(name="wg", bufs=2))
+        wq_pool = ctx.enter_context(tc.tile_pool(name="wq", bufs=3))
         ug_pool = ctx.enter_context(tc.tile_pool(name="ug", bufs=3))
         psum = ctx.enter_context(tc.psum_pool(name="psum", bufs=6))
         psum_c = ctx.enter_context(tc.psum_pool(name="psumc", bufs=2))
@@ -46,14 +50,14 @@ def tile_biaffine_2_pa_kernel(tc, input1, input2, w1, aff1, aff2, bias, out):
         lmat = const.tile([P, NCH, P], BF16)
         x1_raw = const.tile([P, NCH, D], BF16)
         x2_raw = const.tile([P, NCH, D], BF16)
-        x1_g = const.tile([P, NCH * P, PACK], BF16, align_bytes=64)
-        x2_g = const.tile([P, NCH * P, PACK], BF16, align_bytes=64)
-        x1_c = const.tile([P, NCH * P], U32, align_bytes=64)
-        x1_s = const.tile([P, NCH * P], U8, align_bytes=64)
-        x2_c = const.tile([P, NCH * P], U32, align_bytes=64)
-        x2_s = const.tile([P, NCH * P], U8, align_bytes=64)
-        u_c = const.tile([P, O, NCH * P], U32, align_bytes=64)
-        u_s = const.tile([P, O, NCH * P], U8, align_bytes=64)
+        x1_g = const.tile([P, NTOK, PACK], BF16, align_bytes=64)
+        x2_g = const.tile([P, NTOK, PACK], BF16, align_bytes=64)
+        x1_c = const.tile([P, NTOK], U32, align_bytes=64)
+        x1_s = const.tile([P, NTOK], U8, align_bytes=64)
+        x2_c = const.tile([P, NTOK], U32, align_bytes=64)
+        x2_s = const.tile([P, NTOK], U8, align_bytes=64)
+        u_c = const.tile([P, O * NTOK], U32, align_bytes=64)
+        u_s = const.tile([P, O * NTOK], U8, align_bytes=64)
         osb = [const.tile([P, L * O], F32, name="osb%d" % c) for c in range(NCH)]
 
         w_view = w1.rearrange("(t p) o j -> p t o j", p=P)
@@ -61,29 +65,47 @@ def tile_biaffine_2_pa_kernel(tc, input1, input2, w1, aff1, aff2, bias, out):
         w_g = {}
         w_q = {}
         u_g = {}
+        w_group_of = {}
+        u_group_of = {}
+        for k in range(len(W_GROUPS)):
+            for o in W_GROUPS[k]:
+                w_group_of[o] = k
+        for k in range(len(U_GROUPS)):
+            for o in U_GROUPS[k]:
+                u_group_of[o] = k
 
-        def load_w(o):
-            wr = wraw_pool.tile([P, PACK, D], BF16, name="wr", tag="wr")
-            nc.sync.dma_start(out=wr[:], in_=w_view[:, :, o, :])
-            w_raw[o] = wr
+        def load_w(k):
+            n = len(W_GROUPS[k])
+            o0 = W_GROUPS[k][0]
+            wr = wraw_pool.tile([P, PACK, 2, D], BF16, name="wr", tag="wr")
+            nc.sync.dma_start(out=wr[:, :, 0:n, :], in_=w_view[:, :, o0:o0 + n, :])
+            w_raw[k] = wr
 
-        def regroup_w(o):
-            wg = wg_pool.tile([P, D, PACK], BF16, name="wg", tag="wg", align_bytes=64)
+        def regroup_w(k):
+            if k >= len(W_GROUPS):
+                return
+            n = len(W_GROUPS[k])
+            wg = wg_pool.tile([P, 2 * D, PACK], BF16, name="wg", tag="wg", align_bytes=64)
             nc.vector.tensor_copy(
-                out=wg[:].rearrange("p (c i) t -> p c t i", i=4),
-                in_=w_raw[o][:].rearrange("p t (c i) -> p c t i", i=4),
+                out=wg[:, 0:n * D, :].rearrange("p (c i) t -> p c t i", i=4),
+                in_=w_raw[k][:, :, 0:n, :].rearrange("p t n (c i) -> p t (n c) i", i=4).rearrange("p t c i -> p c t i"),
             )
-            w_g[o] = wg
+            w_g[k] = wg
+            if k + W_PREFETCH < len(W_GROUPS):
+                load_w(k + W_PREFETCH)
 
-        def quant_w(o):
-            wc = wq_pool.tile([P, D], U32, name="wc", tag="wc", align_bytes=64)
-            ws = wq_pool.tile([P, D], U8, name="ws", tag="ws", align_bytes=64)
+        def quant_w(k):
+            if k >= len(W_GROUPS):
+                return
+            n = len(W_GROUPS[k])
+            wc = wq_pool.tile([P, 2 * D], U32, name="wc", tag="wc", align_bytes=64)
+            ws = wq_pool.tile([P, 2 * D], U8, name="ws", tag="ws", align_bytes=64)
             nc.vector.quantize_mx(
-                out=wc[:].bitcast(FP8X4),
-                scales=ws[:],
-                in_=w_g[o][:].rearrange("p c t -> p (c t)"),
+                out=wc[:, 0:n * D].bitcast(FP8X4),
+                scales=ws[:, 0:n * D],
+                in_=w_g[k][:, 0:n * D, :].rearrange("p c t -> p (c t)"),
             )
-            w_q[o] = (wc, ws)
+            w_q[k] = (wc, ws)
 
         def transpose_tokens(raw, grouped, c):
             xt = psum.tile([P, PACK, P], BF16, name="xt", tag="acc")
@@ -102,86 +124,97 @@ def tile_biaffine_2_pa_kernel(tc, input1, input2, w1, aff1, aff2, bias, out):
             )
 
         def stage1(o):
-            wc, ws = w_q[o]
-            ug = ug_pool.tile([P, NCH * P, PACK], BF16, name="ug", tag="ug", align_bytes=64)
+            kw = w_group_of[o]
+            wc, ws = w_q[kw]
+            w0 = (o - W_GROUPS[kw][0]) * D
+            ku = u_group_of[o]
+            if o == U_GROUPS[ku][0]:
+                u_g[ku] = ug_pool.tile([P, 2 * NTOK, PACK], BF16, name="ug", tag="ug", align_bytes=64)
+            ug = u_g[ku]
+            r0 = (o - U_GROUPS[ku][0]) * NTOK
             for c in range(NCH):
                 ub = psum.tile([P, PACK, P], F32, name="ub", tag="acc")
                 for t in range(PACK):
                     nc.tensor.matmul_mx(
                         out=ub[:, t, :],
-                        lhsT=wc[:, t * P:(t + 1) * P].bitcast(FP8X4),
-                        lhsT_scale=ws[:, t * P:(t + 1) * P],
+                        lhsT=wc[:, w0 + t * P:w0 + (t + 1) * P].bitcast(FP8X4),
+                        lhsT_scale=ws[:, w0 + t * P:w0 + (t + 1) * P],
                         rhs=x1_c[:, c * P:(c + 1) * P].bitcast(FP8X4),
                         rhs_scale=x1_s[:, c * P:(c + 1) * P],
                         start=True,
                         stop=True,
                     )
+                dst = ug[:, r0 + c * P:r0 + (c + 1) * P, :]
+                src = ub[:].rearrange("p t r -> p r t")
                 if o >= V_EVAC_FROM and c >= 2:
-                    nc.vector.tensor_copy(
-                        out=ug[:, c * P:(c + 1) * P, :],
-                        in_=ub[:].rearrange("p t r -> p r t"),
-                    )
+                    nc.vector.tensor_copy(out=dst, in_=src)
                 else:
-                    nc.scalar.copy(
-                        out=ug[:, c * P:(c + 1) * P, :],
-                        in_=ub[:].rearrange("p t r -> p r t"),
-                    )
-            u_g[o] = ug
+                    nc.scalar.copy(out=dst, in_=src)
 
-        def quant_u(o):
+        def quant_u(k):
+            n = len(U_GROUPS[k])
+            o0 = U_GROUPS[k][0]
             nc.vector.quantize_mx(
-                out=u_c[:, o, :].bitcast(FP8X4),
-                scales=u_s[:, o, :],
-                in_=u_g[o][:].rearrange("p r t -> p (r t)"),
+                out=u_c[:, o0 * NTOK:(o0 + n) * NTOK].bitcast(FP8X4),
+                scales=u_s[:, o0 * NTOK:(o0 + n) * NTOK],
+                in_=u_g[k][:, 0:n * NTOK, :].rearrange("p r t -> p (r t)"),
             )
 
-        def affine_quarter(m, q):
-            c, yh = divmod(m, 2)
-            s = yh * 4 + q
-            cb = psum_c.tile([P, 512], F32, name="cb", tag="cb")
-            nc.tensor.matmul(
-                out=cb[:],
-                lhsT=lmat[:, c, :],
-                rhs=rmat[:, s * 512:(s + 1) * 512],
-                start=True,
-                stop=True,
-            )
-            nc.scalar.copy(out=osb[c][:, s * 512:(s + 1) * 512], in_=cb[:])
+        affine_done = [0]
+
+        def affine_quarters(upto):
+            while affine_done[0] < min(upto, 4 * UNITS):
+                m, q = divmod(affine_done[0], 4)
+                affine_done[0] = affine_done[0] + 1
+                c, yh = divmod(m, 2)
+                s = yh * 4 + q
+                cb = psum_c.tile([P, 512], F32, name="cb", tag="cb")
+                nc.tensor.matmul(
+                    out=cb[:],
+                    lhsT=lmat[:, c, :],
+                    rhs=rmat[:, s * 512:(s + 1) * 512],
+                    start=True,
+                    stop=True,
+                )
+                nc.scalar.copy(out=osb[c][:, s * 512:(s + 1) * 512], in_=cb[:])
 
         def out_view(m):
             c, yh = divmod(m, 2)
             half = L * O // 2
             return osb[c][:, yh * half:(yh + 1) * half].rearrange("p (y o) -> p y o", o=O)
 
-        def stage2_group(m, g):
+        def stage2_passes(m, g):
             c, yh = divmod(m, 2)
             c2 = 2 * (c // 2) + yh
-            ov = out_view(m)
             pb = psum.tile([P, 4, P], F32, name="pb", tag="acc")
             for oo in range(4):
-                o = 4 * g + oo
+                u0 = (4 * g + oo) * NTOK + c * P
                 nc.tensor.matmul_mx(
                     out=pb[:, oo, :],
-                    lhsT=u_c[:, o, c * P:(c + 1) * P].bitcast(FP8X4),
-                    lhsT_scale=u_s[:, o, c * P:(c + 1) * P],
+                    lhsT=u_c[:, u0:u0 + P].bitcast(FP8X4),
+                    lhsT_scale=u_s[:, u0:u0 + P],
                     rhs=x2_c[:, c2 * P:(c2 + 1) * P].bitcast(FP8X4),
                     rhs_scale=x2_s[:, c2 * P:(c2 + 1) * P],
                     start=True,
                     stop=True,
                 )
+            return pb
+
+        def final_add(m, g, pb, y0, y1):
+            ov = out_view(m)
             nc.vector.tensor_tensor(
-                out=ov[:, :, 4 * g:4 * g + 4],
-                in0=pb[:].rearrange("p o y -> p y o"),
-                in1=ov[:, :, 4 * g:4 * g + 4],
+                out=ov[:, y0:y1, 4 * g:4 * g + 4],
+                in0=pb[:, :, y0:y1].rearrange("p o y -> p y o"),
+                in1=ov[:, y0:y1, 4 * g:4 * g + 4],
                 op=ADD,
             )
 
-        def store(m):
+        def store(m, y0, y1):
             c, yh = divmod(m, 2)
             b, h = divmod(c, 2)
             nc.sync.dma_start(
-                out=out[b, h * P:(h + 1) * P, yh * P:(yh + 1) * P, :],
-                in_=out_view(m),
+                out=out[b, h * P:(h + 1) * P, yh * P + y0:yh * P + y1, :],
+                in_=out_view(m)[:, y0:y1, :],
             )
 
         make_identity(nc, ident[:])
@@ -190,8 +223,8 @@ def tile_biaffine_2_pa_kernel(tc, input1, input2, w1, aff1, aff2, bias, out):
         nc.scalar.dma_start(out=bias_bc[:], in_=bias.partition_broadcast(P))
         load_w(0)
         nc.sync.dma_start(out=x1_raw[:], in_=input1.rearrange("b (h p) i -> p (b h) i", p=P))
-        for o in range(1, W_PREFETCH):
-            load_w(o)
+        for k in range(1, W_PREFETCH):
+            load_w(k)
         nc.scalar.dma_start(out=x2_raw[:], in_=input2.rearrange("b (h p) i -> p (b h) i", p=P))
 
         nc.vector.tensor_tensor(out=sel[:], in0=ident[:, 0:O], in1=ident[:, O:2 * O], op=ADD)
@@ -206,65 +239,63 @@ def tile_biaffine_2_pa_kernel(tc, input1, input2, w1, aff1, aff2, bias, out):
         )
         nc.gpsimd.dma_start(out=rmat[2 * O:2 * O + B, :], in_=aff2.rearrange("b y o -> b (y o)"))
 
-        def regroup_and_prefetch(o):
-            regroup_w(o)
-            if o + W_PREFETCH < O:
-                load_w(o + W_PREFETCH)
-
         for c in range(NCH):
             transpose_tokens(x1_raw, x1_g, c)
-        regroup_and_prefetch(0)
+        regroup_w(0)
         quant_w(0)
         quant_tokens(x1_g, x1_c, x1_s, 0, 1)
         quant_tokens(x1_g, x1_c, x1_s, 1, 2)
-        regroup_and_prefetch(1)
+        regroup_w(1)
         quant_tokens(x1_g, x1_c, x1_s, 2, 3)
         quant_tokens(x1_g, x1_c, x1_s, 3, 4)
         quant_w(1)
-        regroup_and_prefetch(2)
+        regroup_w(2)
 
         for s in range(O):
-            if s + REGROUP_AHEAD < O:
-                regroup_and_prefetch(s + REGROUP_AHEAD)
-            if s >= 1:
-                quant_u(s - 1)
-            if s + QUANT_AHEAD < O:
-                quant_w(s + QUANT_AHEAD)
-            if s == 2:
+            k = s // 2
+            if s == 0:
+                quant_w(2)
+            elif s == 1:
+                regroup_w(3)
+            elif s % 2 == 0:
+                quant_u(k - 1)
+                quant_w(k + 2)
+            else:
+                regroup_w(k + 3)
+            if s == 3:
                 nc.vector.tensor_copy(
                     out=a1pad[:, :, O:2 * O],
                     in_=bias_bc[:].unsqueeze(1).to_broadcast([P, NCH, O]),
                 )
                 for b in range(B):
                     nc.vector.memset(a1pad[:, 2 * b:2 * b + 2, 2 * O + b:2 * O + b + 1], 1.0)
-            if 3 <= s < 3 + NCH:
+            if s == 3 or s == 5:
                 transpose_tokens(x2_raw, x2_g, s - 3)
+                transpose_tokens(x2_raw, x2_g, s - 2)
             if s == 7:
                 quant_tokens(x2_g, x2_c, x2_s, 0, NCH)
                 lt = psum.tile([P, NCH, P], BF16, name="lt", tag="acc")
                 for c in range(NCH):
                     nc.tensor.transpose(lt[:, c, :], a1pad[:, c, :], ident[:])
                 nc.scalar.copy(out=lmat[:], in_=lt[:])
-            if 9 <= s < 13:
-                affine_quarter(0, s - 9)
-            if s == 13:
-                affine_quarter(1, 0)
-                affine_quarter(1, 1)
-            if s == 14:
-                affine_quarter(1, 2)
-                stage2_group(0, 0)
-                stage2_group(0, 1)
-            if s == 15:
-                affine_quarter(1, 3)
-                stage2_group(0, 2)
+            if s == O - 1:
+                quant_u(len(U_GROUPS) - 2)
+                affine_quarters(AFFINE_EARLY)
             stage1(s)
-        quant_u(O - 1)
-        stage2_group(0, 3)
-        store(0)
+        quant_u(len(U_GROUPS) - 1)
 
-        for m in range(1, 2 * NCH):
-            for g in range(4):
-                if m + 1 < 2 * NCH:
-                    affine_quarter(m + 1, g)
-                stage2_group(m, g)
-            store(m)
+        for m in range(UNITS):
+            if m < UNITS - 1:
+                for g in range(4):
+                    affine_quarters(4 * m + g + AFFINE_AHEAD + 1)
+                    pb = stage2_passes(m, g)
+                    final_add(m, g, pb, 0, P)
+                store(m, 0, P)
+            else:
+                affine_quarters(4 * UNITS)
+                banks = [stage2_passes(m, g) for g in range(4)]
+                step = P // LAST_SPLIT
+                for y0 in range(0, P, step):
+                    for g in range(4):
+                        final_add(m, g, banks[g], y0, y0 + step)
+                    store(m, y0, y0 + step)

@@ -132,24 +132,26 @@ def tile_biaffine_2_pa_kernel(tc, input1, input2, w1, aff1, aff2, bias, out):
                 u_g[ku] = ug_pool.tile([P, 2 * NTOK, PACK], BF16, name="ug", tag="ug", align_bytes=64)
             ug = u_g[ku]
             r0 = (o - U_GROUPS[ku][0]) * NTOK
-            for c in range(NCH):
-                ub = psum.tile([P, PACK, P], F32, name="ub", tag="acc")
+            for c0 in range(0, NCH, 2):
+                pair = [psum.tile([P, PACK, P], F32, name="ub", tag="acc") for c in (c0, c0 + 1)]
                 for t in range(PACK):
-                    nc.tensor.matmul_mx(
-                        out=ub[:, t, :],
-                        lhsT=wc[:, w0 + t * P:w0 + (t + 1) * P].bitcast(FP8X4),
-                        lhsT_scale=ws[:, w0 + t * P:w0 + (t + 1) * P],
-                        rhs=x1_c[:, c * P:(c + 1) * P].bitcast(FP8X4),
-                        rhs_scale=x1_s[:, c * P:(c + 1) * P],
-                        start=True,
-                        stop=True,
-                    )
-                dst = ug[:, r0 + c * P:r0 + (c + 1) * P, :]
-                src = ub[:].rearrange("p t r -> p r t")
-                if o >= V_EVAC_FROM and c >= 2:
-                    nc.vector.tensor_copy(out=dst, in_=src)
-                else:
-                    nc.scalar.copy(out=dst, in_=src)
+                    for c in (c0, c0 + 1):
+                        nc.tensor.matmul_mx(
+                            out=pair[c - c0][:, t, :],
+                            lhsT=wc[:, w0 + t * P:w0 + (t + 1) * P].bitcast(FP8X4),
+                            lhsT_scale=ws[:, w0 + t * P:w0 + (t + 1) * P],
+                            rhs=x1_c[:, c * P:(c + 1) * P].bitcast(FP8X4),
+                            rhs_scale=x1_s[:, c * P:(c + 1) * P],
+                            start=True,
+                            stop=True,
+                        )
+                for c in (c0, c0 + 1):
+                    dst = ug[:, r0 + c * P:r0 + (c + 1) * P, :]
+                    src = pair[c - c0][:].rearrange("p t r -> p r t")
+                    if o >= V_EVAC_FROM and c >= 2:
+                        nc.vector.tensor_copy(out=dst, in_=src)
+                    else:
+                        nc.scalar.copy(out=dst, in_=src)
 
         def quant_u(k):
             n = len(U_GROUPS[k])
@@ -183,22 +185,23 @@ def tile_biaffine_2_pa_kernel(tc, input1, input2, w1, aff1, aff2, bias, out):
             half = L * O // 2
             return osb[c][:, yh * half:(yh + 1) * half].rearrange("p (y o) -> p y o", o=O)
 
-        def stage2_passes(m, g):
+        def stage2_passes(m, g0):
             c, yh = divmod(m, 2)
             c2 = 2 * (c // 2) + yh
-            pb = psum.tile([P, 4, P], F32, name="pb", tag="acc")
+            pair = [psum.tile([P, 4, P], F32, name="pb", tag="acc") for g in (g0, g0 + 1)]
             for oo in range(4):
-                u0 = (4 * g + oo) * NTOK + c * P
-                nc.tensor.matmul_mx(
-                    out=pb[:, oo, :],
-                    lhsT=u_c[:, u0:u0 + P].bitcast(FP8X4),
-                    lhsT_scale=u_s[:, u0:u0 + P],
-                    rhs=x2_c[:, c2 * P:(c2 + 1) * P].bitcast(FP8X4),
-                    rhs_scale=x2_s[:, c2 * P:(c2 + 1) * P],
-                    start=True,
-                    stop=True,
-                )
-            return pb
+                for g in (g0, g0 + 1):
+                    u0 = (4 * g + oo) * NTOK + c * P
+                    nc.tensor.matmul_mx(
+                        out=pair[g - g0][:, oo, :],
+                        lhsT=u_c[:, u0:u0 + P].bitcast(FP8X4),
+                        lhsT_scale=u_s[:, u0:u0 + P],
+                        rhs=x2_c[:, c2 * P:(c2 + 1) * P].bitcast(FP8X4),
+                        rhs_scale=x2_s[:, c2 * P:(c2 + 1) * P],
+                        start=True,
+                        stop=True,
+                    )
+            return pair
 
         def final_add(m, g, pb, y0, y1):
             ov = out_view(m)
@@ -286,14 +289,15 @@ def tile_biaffine_2_pa_kernel(tc, input1, input2, w1, aff1, aff2, bias, out):
 
         for m in range(UNITS):
             if m < UNITS - 1:
-                for g in range(4):
-                    affine_quarters(4 * m + g + AFFINE_AHEAD + 1)
-                    pb = stage2_passes(m, g)
-                    final_add(m, g, pb, 0, P)
+                for g0 in (0, 2):
+                    affine_quarters(4 * m + g0 + AFFINE_AHEAD + 2)
+                    pair = stage2_passes(m, g0)
+                    final_add(m, g0, pair[0], 0, P)
+                    final_add(m, g0 + 1, pair[1], 0, P)
                 store(m, 0, P)
             else:
                 affine_quarters(4 * UNITS)
-                banks = [stage2_passes(m, g) for g in range(4)]
+                banks = stage2_passes(m, 0) + stage2_passes(m, 2)
                 step = P // LAST_SPLIT
                 for y0 in range(0, P, step):
                     for g in range(4):

from contextlib import ExitStack

import concourse.mybir as mybir
from concourse.masks import make_identity

F32 = mybir.dt.float32
BF16 = mybir.dt.bfloat16
U32 = mybir.dt.uint32
U8 = mybir.dt.uint8
I32 = mybir.dt.int32
FP8X4 = mybir.dt.float8_e4m3fn_x4
ADD = mybir.AluOpType.add

B, L, D, O = 2, 256, 512, 16
P = 128
PACK = 4
NCH = (B * L) // P
NTOK = B * L
UNITS = 2 * NCH
FLOPS = 2 * (B * L) * D * (O * D) + 2 * B * (L * O) * D * L

MANUAL = True
W_GROUPS = [[0], [1]] + [[o, o + 1] for o in range(2, O, 2)]
U_GROUPS = [[o, o + 1] for o in range(0, O - 2, 2)] + [[O - 2], [O - 1]]
W_PREFETCH = 3
V_EVAC_FROM = 13
AFFINE_EARLY = 2
AFFINE_AHEAD = 3
LAST_SPLIT = 2


def tile_biaffine_2_pa_kernel(tc, input1, input2, w1, aff1, aff2, bias, out):
    nc = tc.nc
    with ExitStack() as ctx:
        const = ctx.enter_context(tc.tile_pool(name="const", bufs=1))
        wraw_pool = ctx.enter_context(tc.tile_pool(name="wraw", bufs=W_PREFETCH))
        wg_pool = ctx.enter_context(tc.tile_pool(name="wg", bufs=2))
        wq_pool = ctx.enter_context(tc.tile_pool(name="wq", bufs=3))
        ug_pool = ctx.enter_context(tc.tile_pool(name="ug", bufs=3))
        psum = ctx.enter_context(tc.psum_pool(name="psum", bufs=6))
        psum_c = ctx.enter_context(tc.psum_pool(name="psumc", bufs=2))
        if MANUAL:
            ctx.enter_context(tc.manual_schedule())

        ident = const.tile([P, P], BF16)
        a1pad = const.tile([P, NCH, P], BF16)
        bias_bc = const.tile([P, O], BF16)
        sel = const.tile([P, O], BF16)
        rmat = const.tile([P, L * O], BF16)
        lmat = const.tile([P, NCH, P], BF16)
        x1_raw = const.tile([P, NCH, D], BF16)
        x2_raw = const.tile([P, NCH, D], BF16)
        x1_g = const.tile([P, NTOK, PACK], BF16, align_bytes=64)
        x2_g = const.tile([P, NTOK, PACK], BF16, align_bytes=64)
        x1_c = const.tile([P, NTOK], U32, align_bytes=64)
        x1_s = const.tile([P, NTOK], U8, align_bytes=64)
        x2_c = const.tile([P, NTOK], U32, align_bytes=64)
        x2_s = const.tile([P, NTOK], U8, align_bytes=64)
        u_c = const.tile([P, O * NTOK], U32, align_bytes=64)
        u_s = const.tile([P, O * NTOK], U8, align_bytes=64)
        osb = [const.tile([P, L * O], F32, name="osb%d" % c) for c in range(NCH)]

        w_view = w1.rearrange("(t p) o j -> p t o j", p=P)
        w_raw = {}
        w_g = {}
        w_q = {}
        u_g = {}
        w_group_of = {}
        u_group_of = {}
        for k in range(len(W_GROUPS)):
            for o in W_GROUPS[k]:
                w_group_of[o] = k
        for k in range(len(U_GROUPS)):
            for o in U_GROUPS[k]:
                u_group_of[o] = k

        def load_w(k):
            n = len(W_GROUPS[k])
            o0 = W_GROUPS[k][0]
            wr = wraw_pool.tile([P, PACK, 2, D], BF16, name="wr", tag="wr")
            nc.sync.dma_start(out=wr[:, :, 0:n, :], in_=w_view[:, :, o0:o0 + n, :])
            w_raw[k] = wr

        def regroup_w(k):
            if k >= len(W_GROUPS):
                return
            n = len(W_GROUPS[k])
            wg = wg_pool.tile([P, 2 * D, PACK], BF16, name="wg", tag="wg", align_bytes=64)
            nc.vector.tensor_copy(
                out=wg[:, 0:n * D, :].rearrange("p (c i) t -> p c t i", i=4),
                in_=w_raw[k][:, :, 0:n, :].rearrange("p t n (c i) -> p t (n c) i", i=4).rearrange("p t c i -> p c t i"),
            )
            w_g[k] = wg
            if k + W_PREFETCH < len(W_GROUPS):
                load_w(k + W_PREFETCH)

        def quant_w(k):
            if k >= len(W_GROUPS):
                return
            n = len(W_GROUPS[k])
            wc = wq_pool.tile([P, 2 * D], U32, name="wc", tag="wc", align_bytes=64)
            ws = wq_pool.tile([P, 2 * D], U8, name="ws", tag="ws", align_bytes=64)
            nc.vector.quantize_mx(
                out=wc[:, 0:n * D].bitcast(FP8X4),
                scales=ws[:, 0:n * D],
                in_=w_g[k][:, 0:n * D, :].rearrange("p c t -> p (c t)"),
            )
            w_q[k] = (wc, ws)

        def transpose_tokens(raw, grouped, c):
            xt = psum.tile([P, PACK, P], BF16, name="xt", tag="acc")
            for t in range(PACK):
                nc.tensor.transpose(xt[:, t, :], raw[:, c, t * P:(t + 1) * P], ident[:])
            nc.scalar.copy(
                out=grouped[:, c * P:(c + 1) * P, :],
                in_=xt[:].rearrange("p t r -> p r t"),
            )

        def quant_tokens(grouped, codes, scales, c0, c1):
            nc.vector.quantize_mx(
                out=codes[:, c0 * P:c1 * P].bitcast(FP8X4),
                scales=scales[:, c0 * P:c1 * P],
                in_=grouped[:, c0 * P:c1 * P, :].rearrange("p r t -> p (r t)"),
            )

        def stage1(o):
            kw = w_group_of[o]
            wc, ws = w_q[kw]
            w0 = (o - W_GROUPS[kw][0]) * D
            ku = u_group_of[o]
            if o == U_GROUPS[ku][0]:
                u_g[ku] = ug_pool.tile([P, 2 * NTOK, PACK], BF16, name="ug", tag="ug", align_bytes=64)
            ug = u_g[ku]
            r0 = (o - U_GROUPS[ku][0]) * NTOK
            for c0 in range(0, NCH, 2):
                pair = [psum.tile([P, PACK, P], F32, name="ub", tag="acc") for c in (c0, c0 + 1)]
                for t in range(PACK):
                    for c in (c0, c0 + 1):
                        nc.tensor.matmul_mx(
                            out=pair[c - c0][:, t, :],
                            lhsT=wc[:, w0 + t * P:w0 + (t + 1) * P].bitcast(FP8X4),
                            lhsT_scale=ws[:, w0 + t * P:w0 + (t + 1) * P],
                            rhs=x1_c[:, c * P:(c + 1) * P].bitcast(FP8X4),
                            rhs_scale=x1_s[:, c * P:(c + 1) * P],
                            start=True,
                            stop=True,
                        )
                for c in (c0, c0 + 1):
                    dst = ug[:, r0 + c * P:r0 + (c + 1) * P, :]
                    src = pair[c - c0][:].rearrange("p t r -> p r t")
                    if o >= V_EVAC_FROM and c >= 2:
                        nc.vector.tensor_copy(out=dst, in_=src)
                    else:
                        nc.scalar.copy(out=dst, in_=src)

        def quant_u(k):
            n = len(U_GROUPS[k])
            o0 = U_GROUPS[k][0]
            nc.vector.quantize_mx(
                out=u_c[:, o0 * NTOK:(o0 + n) * NTOK].bitcast(FP8X4),
                scales=u_s[:, o0 * NTOK:(o0 + n) * NTOK],
                in_=u_g[k][:, 0:n * NTOK, :].rearrange("p r t -> p (r t)"),
            )

        affine_done = [0]

        def affine_quarters(upto):
            while affine_done[0] < min(upto, 4 * UNITS):
                m, q = divmod(affine_done[0], 4)
                affine_done[0] = affine_done[0] + 1
                c, yh = divmod(m, 2)
                s = yh * 4 + q
                cb = psum_c.tile([P, 512], F32, name="cb", tag="cb")
                nc.tensor.matmul(
                    out=cb[:],
                    lhsT=lmat[:, c, :],
                    rhs=rmat[:, s * 512:(s + 1) * 512],
                    start=True,
                    stop=True,
                )
                nc.scalar.copy(out=osb[c][:, s * 512:(s + 1) * 512], in_=cb[:])

        def out_view(m):
            c, yh = divmod(m, 2)
            half = L * O // 2
            return osb[c][:, yh * half:(yh + 1) * half].rearrange("p (y o) -> p y o", o=O)

        def stage2_passes(m, g0):
            c, yh = divmod(m, 2)
            c2 = 2 * (c // 2) + yh
            pair = [psum.tile([P, 4, P], F32, name="pb", tag="acc") for g in (g0, g0 + 1)]
            for oo in range(4):
                for g in (g0, g0 + 1):
                    u0 = (4 * g + oo) * NTOK + c * P
                    nc.tensor.matmul_mx(
                        out=pair[g - g0][:, oo, :],
                        lhsT=u_c[:, u0:u0 + P].bitcast(FP8X4),
                        lhsT_scale=u_s[:, u0:u0 + P],
                        rhs=x2_c[:, c2 * P:(c2 + 1) * P].bitcast(FP8X4),
                        rhs_scale=x2_s[:, c2 * P:(c2 + 1) * P],
                        start=True,
                        stop=True,
                    )
            return pair

        def final_add(m, g, pb, y0, y1):
            ov = out_view(m)
            nc.vector.tensor_tensor(
                out=ov[:, y0:y1, 4 * g:4 * g + 4],
                in0=pb[:, :, y0:y1].rearrange("p o y -> p y o"),
                in1=ov[:, y0:y1, 4 * g:4 * g + 4],
                op=ADD,
            )

        def store(m, y0, y1):
            c, yh = divmod(m, 2)
            b, h = divmod(c, 2)
            nc.sync.dma_start(
                out=out[b, h * P:(h + 1) * P, yh * P + y0:yh * P + y1, :],
                in_=out_view(m)[:, y0:y1, :],
            )

        make_identity(nc, ident[:])
        nc.vector.memset(a1pad[:].bitcast(I32), 0)
        nc.scalar.dma_start(out=a1pad[:, :, 0:O], in_=aff1.rearrange("b (h p) o -> p (b h) o", p=P))
        nc.scalar.dma_start(out=bias_bc[:], in_=bias.partition_broadcast(P))
        load_w(0)
        nc.sync.dma_start(out=x1_raw[:], in_=input1.rearrange("b (h p) i -> p (b h) i", p=P))
        for k in range(1, W_PREFETCH):
            load_w(k)
        nc.scalar.dma_start(out=x2_raw[:], in_=input2.rearrange("b (h p) i -> p (b h) i", p=P))

        nc.vector.tensor_tensor(out=sel[:], in0=ident[:, 0:O], in1=ident[:, O:2 * O], op=ADD)
        rview = rmat[:].rearrange("p (y o) -> p y o", o=O)
        nc.vector.tensor_copy(
            out=rview[:, 0:L // 2, :],
            in_=sel[:].unsqueeze(1).to_broadcast([P, L // 2, O]),
        )
        nc.scalar.copy(
            out=rview[:, L // 2:L, :],
            in_=sel[:].unsqueeze(1).to_broadcast([P, L // 2, O]),
        )
        nc.gpsimd.dma_start(out=rmat[2 * O:2 * O + B, :], in_=aff2.rearrange("b y o -> b (y o)"))

        for c in range(NCH):
            transpose_tokens(x1_raw, x1_g, c)
        regroup_w(0)
        quant_w(0)
        quant_tokens(x1_g, x1_c, x1_s, 0, 1)
        quant_tokens(x1_g, x1_c, x1_s, 1, 2)
        regroup_w(1)
        quant_tokens(x1_g, x1_c, x1_s, 2, 3)
        quant_tokens(x1_g, x1_c, x1_s, 3, 4)
        quant_w(1)
        regroup_w(2)

        for s in range(O):
            k = s // 2
            if s == 0:
                quant_w(2)
            elif s == 1:
                regroup_w(3)
            elif s % 2 == 0:
                quant_u(k - 1)
                quant_w(k + 2)
            else:
                regroup_w(k + 3)
            if s == 3:
                nc.vector.tensor_copy(
                    out=a1pad[:, :, O:2 * O],
                    in_=bias_bc[:].unsqueeze(1).to_broadcast([P, NCH, O]),
                )
                for b in range(B):
                    nc.vector.memset(a1pad[:, 2 * b:2 * b + 2, 2 * O + b:2 * O + b + 1], 1.0)
            if s == 3 or s == 5:
                transpose_tokens(x2_raw, x2_g, s - 3)
                transpose_tokens(x2_raw, x2_g, s - 2)
            if s == 7:
                quant_tokens(x2_g, x2_c, x2_s, 0, NCH)
                lt = psum.tile([P, NCH, P], BF16, name="lt", tag="acc")
                for c in range(NCH):
                    nc.tensor.transpose(lt[:, c, :], a1pad[:, c, :], ident[:])
                nc.scalar.copy(out=lmat[:], in_=lt[:])
            if s == O - 1:
                quant_u(len(U_GROUPS) - 2)
                affine_quarters(AFFINE_EARLY)
            stage1(s)
        quant_u(len(U_GROUPS) - 1)

        for m in range(UNITS):
            if m < UNITS - 1:
                for g0 in (0, 2):
                    affine_quarters(4 * m + g0 + AFFINE_AHEAD + 2)
                    pair = stage2_passes(m, g0)
                    final_add(m, g0, pair[0], 0, P)
                    final_add(m, g0 + 1, pair[1], 0, P)
                store(m, 0, P)
            else:
                affine_quarters(4 * UNITS)
                banks = stage2_passes(m, 0) + stage2_passes(m, 2)
                step = P // LAST_SPLIT
                for y0 in range(0, P, step):
                    for g in range(4):
                        final_add(m, g, banks[g], y0, y0 + step)
                    store(m, y0, y0 + step)
